import numpy as np
import ml_dtypes


def mxq(x, axis, fmt="e4m3"):
    dtype, down = {"e4m3": (ml_dtypes.float8_e4m3fn, 7), "e5m2": (ml_dtypes.float8_e5m2, 14)}[fmt]
    v = np.moveaxis(np.asarray(x, np.float32).astype(ml_dtypes.bfloat16).astype(np.float64), axis, -1)
    blocks = v.reshape(v.shape[:-1] + (-1, 32))
    amax = np.abs(blocks).max(-1, keepdims=True)
    byte = np.maximum(np.where(amax > 0, np.frexp(amax)[1] - 1 + 127, 0) - down, 1)
    scale = np.exp2(byte - 127.0)
    codes = (blocks / scale).astype(np.float32).astype(dtype).astype(np.float64)
    return np.moveaxis((codes * scale).reshape(v.shape), -1, axis)


WIDE = False


def mx_kscale(k):
    if not WIDE:
        return np.ones(k)
    levels = np.array([10, -10, 5, -5, 0])
    a = np.random.permutation(np.resize(levels, k // 512 * 4)).reshape(k // 512, 4)
    idx = np.arange(k)
    return np.exp2(a[idx // 512, idx % 128 // 32])


BF16 = ml_dtypes.bfloat16


def bf(x):
    return np.asarray(x, np.float32).astype(BF16)


def f64(x):
    return np.asarray(x).astype(np.float64)


B, O, A, H, Z = 256, 512, 512, 1536, 512
CLAMP = 10.0
LV_LO, LV_HI = -12.0, 2.0


def setup_inputs():
    s, t = mx_kscale(O + H), mx_kscale(H)
    return {
        "x_t": bf(np.random.standard_normal((B, O)) * s[:O]),
        "h_prev": bf(np.random.standard_normal((B, H)) * s[O:]),
        "eps": bf(np.random.standard_normal((B, Z))),
        "enc_w1": bf(np.random.standard_normal((H, O + H)) / np.sqrt(O + H) * t[:, None] / s[None, :]),
        "enc_b1": bf(np.random.standard_normal(H) * 0.1 * t),
        "enc_w2": bf(np.random.standard_normal((2 * Z, H)) * 1.4 / np.sqrt(H) / t[None, :]),
        "enc_b2": bf(np.concatenate([np.random.standard_normal(Z) * 0.1, np.random.uniform(LV_LO, LV_HI, Z)])),
        "mu_p": bf(np.random.standard_normal((B, Z)) * 0.7),
        "logvar_p": bf(np.random.standard_normal((B, Z)) * 0.7),
    }


def reference(x_t, h_prev, eps, enc_w1, enc_b1, enc_w2, enc_b2, mu_p, logvar_p):
    mu_p, logvar_p = f64(mu_p), f64(logvar_p)
    xh = np.concatenate([f64(x_t), f64(h_prev)], -1)
    hid = np.maximum((mxq(xh, 1, "e4m3") @ mxq(f64(enc_w1), 1, "e4m3").T) + f64(enc_b1), 0.0)
    stats = (mxq(hid, 1, "e4m3") @ mxq(f64(enc_w2), 1, "e4m3").T) + f64(enc_b2)
    mu_q = stats[:, :Z]
    logvar_q = np.clip(stats[:, Z:], -CLAMP, CLAMP)
    std_q = np.exp(0.5 * logvar_q)
    z_t = mu_q + f64(eps) * std_q
    var_p = np.exp(logvar_p)
    kl = 0.5 * np.sum((mu_q - mu_p) ** 2 / var_p + np.exp(logvar_q) / var_p + (logvar_p - logvar_q) - 1.0, axis=-1)
    return z_t, mu_q, logvar_q, kl

@@ -1,0 +1,306 @@
+from contextlib import ExitStack
+
+import concourse.mybir as mybir
+from concourse.masks import make_identity
+
+F32 = mybir.dt.float32
+BF16 = mybir.dt.bfloat16
+U32 = mybir.dt.uint32
+U8 = mybir.dt.uint8
+FP8X4 = mybir.dt.float8_e4m3fn_x4
+ACT = mybir.ActivationFunctionType
+ALU = mybir.AluOpType
+AXIS = mybir.AxisListType
+
+P = 128
+K_PASS = 4 * P
+PAIR = 2 * P
+
+B, O, H, Z = 256, 512, 1536, 512
+K1 = O + H
+PASSES1 = K1 // K_PASS
+PASSES2 = H // K_PASS
+W1_PAIRS = H // PAIR
+W2_PAIRS = 2 * Z // PAIR
+B_TILES = B // P
+Z_PARTS = Z // PAIR
+CLAMP = 10.0
+
+FLOPS = 2 * B * K1 * H + 2 * B * H * 2 * Z
+
+
+def tile_vrnncell_pa_kernel(
+    tc, x_t, h_prev, eps, enc_w1, enc_b1, enc_w2, enc_b2, mu_p, logvar_p, out_0, out_1, out_2, out_3
+):
+    nc = tc.nc
+    with ExitStack() as ctx:
+        keep = ctx.enter_context(tc.tile_pool(name="keep", bufs=1))
+        stage = ctx.enter_context(tc.tile_pool(name="stage", bufs=6))
+        psum_t = ctx.enter_context(tc.psum_pool(name="psum_t", bufs=4))
+        psum_h = ctx.enter_context(tc.psum_pool(name="psum_h", bufs=2))
+        psum_s = ctx.enter_context(tc.psum_pool(name="psum_s", bufs=2))
+
+        def load_pair(rows, width, name):
+            raw = keep.tile([P, 2 * width], BF16, name=name)
+            nc.sync.dma_start(out=raw[:], in_=rows.rearrange("(p a) k -> p (a k)", a=2))
+            return raw[:].bitcast(F32).rearrange("p (a w) -> p a w", a=2)
+
+        x_words = load_pair(x_t, O, "x_raw")
+        h_words = load_pair(h_prev, H, "h_raw")
+        w1_words = [
+            load_pair(enc_w1[c * PAIR : (c + 1) * PAIR, :], K1, "w1_raw%d" % c) for c in range(W1_PAIRS)
+        ]
+
+        def load_prior(src, name):
+            prior = keep.tile([P, B_TILES, Z], BF16, name=name)
+            nc.sync.dma_start(out=prior[:], in_=src.rearrange("(t p) z -> p t z", p=P))
+            return prior
+
+        lvp_sb = load_prior(logvar_p, "lvp_sb")
+        mup_sb = load_prior(mu_p, "mup_sb")
+        eps_sb = load_prior(eps, "eps_sb")
+        w2_words = [
+            load_pair(enc_w2[q * PAIR : (q + 1) * PAIR, :], H, "w2_raw%d" % q) for q in range(W2_PAIRS)
+        ]
+
+        ident = keep.tile([P, P], F32)
+        make_identity(nc, ident[:])
+        ones = keep.tile([P, P], BF16)
+        nc.gpsimd.memset(ones[:], 1.0)
+        b1_rows = keep.tile([P, P], F32)
+        nc.gpsimd.memset(b1_rows[:], 0.0)
+        nc.scalar.dma_start(
+            out=b1_rows[:].bitcast(BF16)[0:W1_PAIRS, :], in_=enc_b1.rearrange("(c w) -> c w", c=W1_PAIRS)
+        )
+        b2_row = keep.tile([P, 2 * Z], BF16)
+        nc.gpsimd.memset(b2_row[:], 0.0)
+        nc.scalar.dma_start(out=b2_row[0:1, :], in_=enc_b2.rearrange("(o n) -> o n", o=1))
+        kl_cols = keep.tile([P, P], F32)
+        nc.gpsimd.memset(kl_cols[:], 0.0)
+
+        warm = keep.tile([P, 1], F32)
+        nc.vector.memset(warm[:], 0.0)
+        nc.scalar.activation(out=warm[:], in_=warm[:], func=ACT.Exp)
+
+        x_codes = keep.tile([P, PASSES1, B], U32, align_bytes=64)
+        x_scales = keep.tile([P, PASSES1, B], U8, align_bytes=64)
+        w1_codes = keep.tile([P, W1_PAIRS, PASSES1, PAIR], U32, align_bytes=64)
+        w1_scales = keep.tile([P, W1_PAIRS, PASSES1, PAIR], U8, align_bytes=64)
+        hid_codes = keep.tile([P, PASSES2, B], U32, align_bytes=64)
+        hid_scales = keep.tile([P, PASSES2, B], U8, align_bytes=64)
+        w2_codes = keep.tile([P, W2_PAIRS, PASSES2, PAIR], U32, align_bytes=64)
+        w2_scales = keep.tile([P, W2_PAIRS, PASSES2, PAIR], U8, align_bytes=64)
+
+        def transpose_pass(words, g):
+            bank = psum_t.tile([P, 4 * P], F32)
+            for a in range(2):
+                for u in range(2):
+                    nc.tensor.transpose(
+                        out=bank[:, (2 * a + u) * P : (2 * a + u + 1) * P],
+                        in_=words[:, a, (2 * g + u) * P : (2 * g + u + 1) * P],
+                        identity=ident[:],
+                    )
+            return bank
+
+        def group_rows_in_order(copy, bank):
+            grouped = stage.tile([P, 4 * PAIR], BF16, align_bytes=64)
+            copy(
+                out=grouped[:].bitcast(F32).rearrange("p (r a u) -> p r a u", a=2, u=2),
+                in_=bank[:].rearrange("p (a u r) -> p r a u", a=2, u=2),
+            )
+            return grouped
+
+        def group_rows_even_odd(copy, bank):
+            grouped = stage.tile([P, 4 * PAIR], BF16, align_bytes=64)
+            copy(
+                out=grouped[:].bitcast(F32).rearrange("p (a r u) -> p a r u", a=2, u=2),
+                in_=bank[:].rearrange("p (a u r) -> p a r u", a=2, u=2),
+            )
+            return grouped
+
+        def quantise(grouped, codes, scales):
+            nc.vector.quantize_mx(out=codes.bitcast(FP8X4), scales=scales, in_=grouped[:])
+
+        x_banks = [transpose_pass(x_words, 0)] + [transpose_pass(h_words, g) for g in range(PASSES1 - 1)]
+        x_grouped = [
+            group_rows_in_order(nc.vector.tensor_copy if g % 2 == 0 else nc.scalar.copy, x_banks[g])
+            for g in range(PASSES1)
+        ]
+        for g in range(PASSES1):
+            quantise(x_grouped[g], x_codes[:, g, :], x_scales[:, g, :])
+
+        b1_bank = psum_h.tile([P, 4 * P], F32, tag="hid_acc")
+        nc.tensor.transpose(out=b1_bank[:, 0:P], in_=b1_rows[:], identity=ident[:])
+        b1_cols = keep.tile([P, 2 * W1_PAIRS], F32)
+        nc.vector.tensor_copy(out=b1_cols[:], in_=b1_bank[:].bitcast(BF16)[:, 0 : 2 * W1_PAIRS])
+
+        b2_all = keep.tile([P, 2 * Z], F32)
+        for half in range(2):
+            b2_bank = psum_s.tile([P, Z], F32, tag="stats_acc")
+            nc.tensor.matmul(
+                out=b2_bank[:], lhsT=ones[:], rhs=b2_row[:, half * Z : (half + 1) * Z], start=True, stop=True
+            )
+            nc.vector.tensor_copy(out=b2_all[:, half * Z : (half + 1) * Z], in_=b2_bank[:])
+
+        hid_rows = keep.tile([P, 2 * W1_PAIRS, B], BF16)
+
+        def prepare_w1(c):
+            banks = [transpose_pass(w1_words[c], g) for g in range(PASSES1)]
+            grouped = [
+                group_rows_even_odd(nc.vector.tensor_copy if g == 0 else nc.scalar.copy, banks[g])
+                for g in range(PASSES1)
+            ]
+            for g in range(PASSES1):
+                quantise(grouped[g], w1_codes[:, c, g, :], w1_scales[:, c, g, :])
+
+        def layer1(c):
+            hid_acc = psum_h.tile([P, 2, B], F32)
+            for e in range(2):
+                for g in range(PASSES1):
+                    nc.tensor.matmul_mx(
+                        out=hid_acc[:, e, :],
+                        lhsT=w1_codes[:, c, g, e * P : (e + 1) * P].bitcast(FP8X4),
+                        lhsT_scale=w1_scales[:, c, g, e * P : (e + 1) * P],
+                        rhs=x_codes[:, g, :].bitcast(FP8X4),
+                        rhs_scale=x_scales[:, g, :],
+                        start=(g == 0),
+                        stop=(g == PASSES1 - 1),
+                    )
+            for e in range(2):
+                nc.scalar.activation(
+                    out=hid_rows[:, 2 * c + e, :],
+                    in_=hid_acc[:, e, :],
+                    func=ACT.Relu,
+                    bias=b1_cols[:, 2 * c + e : 2 * c + e + 1],
+                )
+
+        def quantise_hid(g):
+            hid_grouped = stage.tile([P, 4 * B], BF16, align_bytes=64, tag="grouped")
+            nc.vector.tensor_copy(
+                out=hid_grouped[:].rearrange("p (b t) -> p b t", t=4),
+                in_=hid_rows[:, 4 * g : 4 * g + 4, :].rearrange("p t b -> p b t"),
+            )
+            quantise(hid_grouped, hid_codes[:, g, :], hid_scales[:, g, :])
+
+        prepare_w1(0)
+        for c in range(1, W1_PAIRS):
+            prepare_w1(c)
+            layer1(c - 1)
+            if c % 2 == 0:
+                quantise_hid(c // 2 - 1)
+
+        inv_std_p = keep.tile([P, B_TILES, Z], F32)
+        nc.scalar.activation(out=inv_std_p[:], in_=lvp_sb[:], func=ACT.Exp, scale=-0.5)
+
+        mu_q = keep.tile([P, B_TILES, Z], F32)
+        lv_q = keep.tile([P, B_TILES, Z], F32)
+        std_q = keep.tile([P, B_TILES, Z], F32)
+        z_sb = keep.tile([P, B_TILES, Z], F32)
+        dev = keep.tile([P, B_TILES, Z], F32)
+        lv_diff = keep.tile([P, B_TILES, Z], F32)
+        dev_sq = keep.tile([P, B_TILES, Z], BF16)
+        var_ratio = keep.tile([P, B_TILES, Z], BF16)
+        sum_dev_sq = keep.tile([P, B_TILES, Z_PARTS], F32)
+        sum_var_ratio = keep.tile([P, B_TILES, Z_PARTS], F32)
+        sum_lv_diff = keep.tile([P, B_TILES, Z_PARTS], F32)
+
+        def prepare_w2(q):
+            banks = [transpose_pass(w2_words[q], g) for g in range(PASSES2)]
+            grouped = [group_rows_in_order(nc.scalar.copy, banks[g]) for g in range(PASSES2)]
+            for g in range(PASSES2):
+                quantise(grouped[g], w2_codes[:, q, g, :], w2_scales[:, q, g, :])
+
+        def layer2(q):
+            stats_acc = psum_s.tile([P, B_TILES, PAIR], F32)
+            for t in range(B_TILES):
+                for g in range(PASSES2):
+                    nc.tensor.matmul_mx(
+                        out=stats_acc[:, t, :],
+                        lhsT=hid_codes[:, g, t * P : (t + 1) * P].bitcast(FP8X4),
+                        lhsT_scale=hid_scales[:, g, t * P : (t + 1) * P],
+                        rhs=w2_codes[:, q, g, :].bitcast(FP8X4),
+                        rhs_scale=w2_scales[:, q, g, :],
+                        start=(g == 0),
+                        stop=(g == PASSES2 - 1),
+                    )
+            return stats_acc
+
+        def bias2(q):
+            return b2_all[:, q * PAIR : (q + 1) * PAIR].unsqueeze(1).to_broadcast([P, B_TILES, PAIR])
+
+        def store(out, tile, cols):
+            nc.sync.dma_start(out=out.rearrange("(t p) z -> p t z", p=P)[:, :, cols], in_=tile[:, :, cols])
+
+        def finish_mu(part, stats_acc):
+            cols = slice(part * PAIR, (part + 1) * PAIR)
+            nc.vector.tensor_tensor(out=mu_q[:, :, cols], in0=stats_acc[:], in1=bias2(part), op=ALU.add)
+            store(out_1, mu_q, cols)
+            nc.vector.tensor_tensor(out=dev[:, :, cols], in0=mu_q[:, :, cols], in1=mup_sb[:, :, cols], op=ALU.subtract)
+            nc.vector.tensor_tensor(out=dev[:, :, cols], in0=dev[:, :, cols], in1=inv_std_p[:, :, cols], op=ALU.mult)
+            for t in range(B_TILES):
+                nc.scalar.activation(
+                    out=dev_sq[:, t, cols],
+                    in_=dev[:, t, cols],
+                    func=ACT.Square,
+                    accum_out=sum_dev_sq[:, t, part : part + 1],
+                )
+
+        def finish_logvar(part, stats_acc):
+            cols = slice(part * PAIR, (part + 1) * PAIR)
+            nc.vector.tensor_tensor(
+                out=lv_q[:, :, cols], in0=stats_acc[:], in1=bias2(Z_PARTS + part), op=ALU.add
+            )
+            nc.vector.tensor_scalar(
+                out=lv_q[:, :, cols], in0=lv_q[:, :, cols], scalar1=CLAMP, scalar2=-CLAMP, op0=ALU.min, op1=ALU.max
+            )
+            store(out_2, lv_q, cols)
+            nc.scalar.activation(out=std_q[:, :, cols], in_=lv_q[:, :, cols], func=ACT.Exp, scale=0.5)
+            for t in range(B_TILES):
+                nc.vector.scalar_tensor_tensor(
+                    out=lv_diff[:, t, cols],
+                    in0=lv_q[:, t, cols],
+                    scalar=1.0,
+                    in1=lvp_sb[:, t, cols],
+                    op0=ALU.mult,
+                    op1=ALU.subtract,
+                    accum_out=sum_lv_diff[:, t, part : part + 1],
+                )
+            nc.vector.tensor_tensor(out=z_sb[:, :, cols], in0=std_q[:, :, cols], in1=eps_sb[:, :, cols], op=ALU.mult)
+            nc.vector.tensor_tensor(out=z_sb[:, :, cols], in0=z_sb[:, :, cols], in1=mu_q[:, :, cols], op=ALU.add)
+            store(out_0, z_sb, cols)
+            for t in range(B_TILES):
+                nc.scalar.activation(
+                    out=var_ratio[:, t, cols],
+                    in_=lv_diff[:, t, cols],
+                    func=ACT.Exp,
+                    accum_out=sum_var_ratio[:, t, part : part + 1],
+                )
+
+        def finish(q):
+            stats_acc = layer2(q)
+            if q < Z_PARTS:
+                finish_mu(q, stats_acc)
+            else:
+                finish_logvar(q - Z_PARTS, stats_acc)
+
+        prepare_w2(0)
+        layer1(W1_PAIRS - 1)
+        quantise_hid(PASSES2 - 1)
+        for q in range(1, W2_PAIRS):
+            prepare_w2(q)
+            finish(q - 1)
+        finish(W2_PAIRS - 1)
+
+        kl_parts = keep.tile([P, B_TILES, Z_PARTS], F32)
+        nc.vector.tensor_tensor(out=kl_parts[:], in0=sum_dev_sq[:], in1=sum_var_ratio[:], op=ALU.add)
+        nc.vector.tensor_tensor(out=kl_parts[:], in0=kl_parts[:], in1=sum_lv_diff[:], op=ALU.subtract)
+        kl_sum = keep.tile([P, B_TILES], F32)
+        nc.vector.tensor_reduce(out=kl_sum[:], in_=kl_parts[:], axis=AXIS.X, op=ALU.add)
+        nc.vector.tensor_scalar(
+            out=kl_cols[:, 0:B_TILES], in0=kl_sum[:], scalar1=0.5, scalar2=-0.5 * Z, op0=ALU.mult, op1=ALU.add
+        )
+        kl_bank = psum_t.tile([P, 4 * P], F32, tag="bank")
+        nc.tensor.transpose(out=kl_bank[:, 0:P], in_=kl_cols[:], identity=ident[:])
+        kl_rows = keep.tile([P, P], F32)
+        nc.vector.tensor_copy(out=kl_rows[:], in_=kl_bank[:, 0:P])
+        nc.sync.dma_start(out=out_3.rearrange("(t p) -> t p", p=P), in_=kl_rows[0:B_TILES, :])

@@ -39,6 +39,7 @@ def tile_vrnncell_pa_kernel(
         psum_t = ctx.enter_context(tc.psum_pool(name="psum_t", bufs=4))
         psum_h = ctx.enter_context(tc.psum_pool(name="psum_h", bufs=2))
         psum_s = ctx.enter_context(tc.psum_pool(name="psum_s", bufs=2))
+        ctx.enter_context(tc.manual_schedule())
 
         def load_pair(rows, width, name):
             raw = keep.tile([P, 2 * width], BF16, name=name)

@@ -25,6 +25,7 @@ W2_PAIRS = 2 * Z // PAIR
 B_TILES = B // P
 Z_PARTS = Z // PAIR
 CLAMP = 10.0
+PREPARE_AHEAD = 2
 
 FLOPS = 2 * B * K1 * H + 2 * B * H * 2 * Z
 
@@ -36,9 +37,8 @@ def tile_vrnncell_pa_kernel(
     with ExitStack() as ctx:
         keep = ctx.enter_context(tc.tile_pool(name="keep", bufs=1))
         stage = ctx.enter_context(tc.tile_pool(name="stage", bufs=6))
-        psum_t = ctx.enter_context(tc.psum_pool(name="psum_t", bufs=4))
-        psum_h = ctx.enter_context(tc.psum_pool(name="psum_h", bufs=2))
-        psum_s = ctx.enter_context(tc.psum_pool(name="psum_s", bufs=2))
+        psum_t = ctx.enter_context(tc.psum_pool(name="psum_t", bufs=6))
+        psum_acc = ctx.enter_context(tc.psum_pool(name="psum_acc", bufs=2))
         ctx.enter_context(tc.manual_schedule())
 
         def load_pair(rows, width, name):
@@ -130,14 +130,14 @@ def tile_vrnncell_pa_kernel(
         for g in range(PASSES1):
             quantise(x_grouped[g], x_codes[:, g, :], x_scales[:, g, :])
 
-        b1_bank = psum_h.tile([P, 4 * P], F32, tag="hid_acc")
+        b1_bank = psum_t.tile([P, 4 * P], F32, tag="bank")
         nc.tensor.transpose(out=b1_bank[:, 0:P], in_=b1_rows[:], identity=ident[:])
         b1_cols = keep.tile([P, 2 * W1_PAIRS], F32)
         nc.vector.tensor_copy(out=b1_cols[:], in_=b1_bank[:].bitcast(BF16)[:, 0 : 2 * W1_PAIRS])
 
         b2_all = keep.tile([P, 2 * Z], F32)
         for half in range(2):
-            b2_bank = psum_s.tile([P, Z], F32, tag="stats_acc")
+            b2_bank = psum_acc.tile([P, Z], F32, tag="acc")
             nc.tensor.matmul(
                 out=b2_bank[:], lhsT=ones[:], rhs=b2_row[:, half * Z : (half + 1) * Z], start=True, stop=True
             )
@@ -155,7 +155,7 @@ def tile_vrnncell_pa_kernel(
                 quantise(grouped[g], w1_codes[:, c, g, :], w1_scales[:, c, g, :])
 
         def layer1(c):
-            hid_acc = psum_h.tile([P, 2, B], F32)
+            hid_acc = psum_acc.tile([P, 2, B], F32, tag="acc")
             for e in range(2):
                 for g in range(PASSES1):
                     nc.tensor.matmul_mx(
@@ -207,12 +207,16 @@ def tile_vrnncell_pa_kernel(
 
         def prepare_w2(q):
             banks = [transpose_pass(w2_words[q], g) for g in range(PASSES2)]
-            grouped = [group_rows_in_order(nc.scalar.copy, banks[g]) for g in range(PASSES2)]
+            vector_helps = q < PREPARE_AHEAD
+            grouped = [
+                group_rows_in_order(nc.vector.tensor_copy if vector_helps and g == 0 else nc.scalar.copy, banks[g])
+                for g in range(PASSES2)
+            ]
             for g in range(PASSES2):
                 quantise(grouped[g], w2_codes[:, q, g, :], w2_scales[:, q, g, :])
 
         def layer2(q):
-            stats_acc = psum_s.tile([P, B_TILES, PAIR], F32)
+            stats_acc = psum_acc.tile([P, B_TILES, PAIR], F32, tag="acc")
             for t in range(B_TILES):
                 for g in range(PASSES2):
                     nc.tensor.matmul_mx(
@@ -238,6 +242,9 @@ def tile_vrnncell_pa_kernel(
             store(out_1, mu_q, cols)
             nc.vector.tensor_tensor(out=dev[:, :, cols], in0=mu_q[:, :, cols], in1=mup_sb[:, :, cols], op=ALU.subtract)
             nc.vector.tensor_tensor(out=dev[:, :, cols], in0=dev[:, :, cols], in1=inv_std_p[:, :, cols], op=ALU.mult)
+
+        def sum_dev_squares(part):
+            cols = slice(part * PAIR, (part + 1) * PAIR)
             for t in range(B_TILES):
                 nc.scalar.activation(
                     out=dev_sq[:, t, cols],
@@ -279,18 +286,21 @@ def tile_vrnncell_pa_kernel(
 
         def finish(q):
             stats_acc = layer2(q)
+            if 1 <= q <= Z_PARTS:
+                sum_dev_squares(q - 1)
             if q < Z_PARTS:
                 finish_mu(q, stats_acc)
             else:
                 finish_logvar(q - Z_PARTS, stats_acc)
 
-        prepare_w2(0)
-        layer1(W1_PAIRS - 1)
-        quantise_hid(PASSES2 - 1)
-        for q in range(1, W2_PAIRS):
-            prepare_w2(q)
-            finish(q - 1)
-        finish(W2_PAIRS - 1)
+        for q in range(W2_PAIRS + PREPARE_AHEAD):
+            if q < W2_PAIRS:
+                prepare_w2(q)
+            if q == 0:
+                layer1(W1_PAIRS - 1)
+                quantise_hid(PASSES2 - 1)
+            if q >= PREPARE_AHEAD:
+                finish(q - PREPARE_AHEAD)
 
         kl_parts = keep.tile([P, B_TILES, Z_PARTS], F32)
         nc.vector.tensor_tensor(out=kl_parts[:], in0=sum_dev_sq[:], in1=sum_var_ratio[:], op=ALU.add)

@@ -10,7 +10,6 @@ U8 = mybir.dt.uint8
 FP8X4 = mybir.dt.float8_e4m3fn_x4
 ACT = mybir.ActivationFunctionType
 ALU = mybir.AluOpType
-AXIS = mybir.AxisListType
 
 P = 128
 K_PASS = 4 * P
@@ -26,6 +25,8 @@ B_TILES = B // P
 Z_PARTS = Z // PAIR
 CLAMP = 10.0
 PREPARE_AHEAD = 2
+KL_TERMS = 3
+DEV_SQ, LV_DIFF, VAR_RATIO = 0, 1, 2
 
 FLOPS = 2 * B * K1 * H + 2 * B * H * 2 * Z
 
@@ -76,8 +77,8 @@ def tile_vrnncell_pa_kernel(
         b2_row = keep.tile([P, 2 * Z], BF16)
         nc.gpsimd.memset(b2_row[:], 0.0)
         nc.scalar.dma_start(out=b2_row[0:1, :], in_=enc_b2.rearrange("(o n) -> o n", o=1))
-        kl_cols = keep.tile([P, P], F32)
-        nc.gpsimd.memset(kl_cols[:], 0.0)
+        kl_sums = keep.tile([P, KL_TERMS * Z_PARTS, P], F32)
+        nc.gpsimd.memset(kl_sums[:], 0.0)
 
         warm = keep.tile([P, 1], F32)
         nc.vector.memset(warm[:], 0.0)
@@ -183,15 +184,18 @@ def tile_vrnncell_pa_kernel(
             )
             quantise(hid_grouped, hid_codes[:, g, :], hid_scales[:, g, :])
 
-        prepare_w1(0)
-        for c in range(1, W1_PAIRS):
-            prepare_w1(c)
-            layer1(c - 1)
-            if c % 2 == 0:
-                quantise_hid(c // 2 - 1)
+        def layer1_and_quantise(c):
+            layer1(c)
+            if c % 2 == 1:
+                quantise_hid(c // 2)
+
+        for c in range(W1_PAIRS + PREPARE_AHEAD - 1):
+            if c < W1_PAIRS:
+                prepare_w1(c)
+            if c >= PREPARE_AHEAD:
+                layer1_and_quantise(c - PREPARE_AHEAD)
 
         inv_std_p = keep.tile([P, B_TILES, Z], F32)
-        nc.scalar.activation(out=inv_std_p[:], in_=lvp_sb[:], func=ACT.Exp, scale=-0.5)
 
         mu_q = keep.tile([P, B_TILES, Z], F32)
         lv_q = keep.tile([P, B_TILES, Z], F32)
@@ -201,9 +205,9 @@ def tile_vrnncell_pa_kernel(
         lv_diff = keep.tile([P, B_TILES, Z], F32)
         dev_sq = keep.tile([P, B_TILES, Z], BF16)
         var_ratio = keep.tile([P, B_TILES, Z], BF16)
-        sum_dev_sq = keep.tile([P, B_TILES, Z_PARTS], F32)
-        sum_var_ratio = keep.tile([P, B_TILES, Z_PARTS], F32)
-        sum_lv_diff = keep.tile([P, B_TILES, Z_PARTS], F32)
+
+        def kl_sum(term, part, t):
+            return kl_sums[:, term * Z_PARTS + part, t : t + 1]
 
         def prepare_w2(q):
             banks = [transpose_pass(w2_words[q], g) for g in range(PASSES2)]
@@ -250,10 +254,10 @@ def tile_vrnncell_pa_kernel(
                     out=dev_sq[:, t, cols],
                     in_=dev[:, t, cols],
                     func=ACT.Square,
-                    accum_out=sum_dev_sq[:, t, part : part + 1],
+                    accum_out=kl_sum(DEV_SQ, part, t),
                 )
 
-        def finish_logvar(part, stats_acc):
+        def clip_logvar(part, stats_acc):
             cols = slice(part * PAIR, (part + 1) * PAIR)
             nc.vector.tensor_tensor(
                 out=lv_q[:, :, cols], in0=stats_acc[:], in1=bias2(Z_PARTS + part), op=ALU.add
@@ -263,55 +267,67 @@ def tile_vrnncell_pa_kernel(
             )
             store(out_2, lv_q, cols)
             nc.scalar.activation(out=std_q[:, :, cols], in_=lv_q[:, :, cols], func=ACT.Exp, scale=0.5)
+
+        def sum_logvar_terms(part):
+            cols = slice(part * PAIR, (part + 1) * PAIR)
             for t in range(B_TILES):
                 nc.vector.scalar_tensor_tensor(
                     out=lv_diff[:, t, cols],
                     in0=lv_q[:, t, cols],
-                    scalar=1.0,
+                    scalar=-1.0,
                     in1=lvp_sb[:, t, cols],
                     op0=ALU.mult,
-                    op1=ALU.subtract,
-                    accum_out=sum_lv_diff[:, t, part : part + 1],
+                    op1=ALU.add,
+                    accum_out=kl_sum(LV_DIFF, part, t),
                 )
-            nc.vector.tensor_tensor(out=z_sb[:, :, cols], in0=std_q[:, :, cols], in1=eps_sb[:, :, cols], op=ALU.mult)
-            nc.vector.tensor_tensor(out=z_sb[:, :, cols], in0=z_sb[:, :, cols], in1=mu_q[:, :, cols], op=ALU.add)
-            store(out_0, z_sb, cols)
             for t in range(B_TILES):
                 nc.scalar.activation(
                     out=var_ratio[:, t, cols],
                     in_=lv_diff[:, t, cols],
                     func=ACT.Exp,
-                    accum_out=sum_var_ratio[:, t, part : part + 1],
+                    scale=-1.0,
+                    accum_out=kl_sum(VAR_RATIO, part, t),
                 )
+
+        def sample(part):
+            cols = slice(part * PAIR, (part + 1) * PAIR)
+            nc.vector.tensor_tensor(out=z_sb[:, :, cols], in0=std_q[:, :, cols], in1=eps_sb[:, :, cols], op=ALU.mult)
+            nc.vector.tensor_tensor(out=z_sb[:, :, cols], in0=z_sb[:, :, cols], in1=mu_q[:, :, cols], op=ALU.add)
+            store(out_0, z_sb, cols)
 
         def finish(q):
             stats_acc = layer2(q)
             if 1 <= q <= Z_PARTS:
                 sum_dev_squares(q - 1)
+            if q > Z_PARTS:
+                sum_logvar_terms(q - Z_PARTS - 1)
             if q < Z_PARTS:
                 finish_mu(q, stats_acc)
             else:
-                finish_logvar(q - Z_PARTS, stats_acc)
+                clip_logvar(q - Z_PARTS, stats_acc)
 
         for q in range(W2_PAIRS + PREPARE_AHEAD):
             if q < W2_PAIRS:
                 prepare_w2(q)
             if q == 0:
-                layer1(W1_PAIRS - 1)
-                quantise_hid(PASSES2 - 1)
+                layer1_and_quantise(W1_PAIRS - 1)
+            if q == PREPARE_AHEAD:
+                nc.scalar.activation(out=inv_std_p[:], in_=lvp_sb[:], func=ACT.Exp, scale=-0.5)
             if q >= PREPARE_AHEAD:
                 finish(q - PREPARE_AHEAD)
+        sum_logvar_terms(Z_PARTS - 1)
+        for part in range(Z_PARTS):
+            sample(part)
 
-        kl_parts = keep.tile([P, B_TILES, Z_PARTS], F32)
-        nc.vector.tensor_tensor(out=kl_parts[:], in0=sum_dev_sq[:], in1=sum_var_ratio[:], op=ALU.add)
-        nc.vector.tensor_tensor(out=kl_parts[:], in0=kl_parts[:], in1=sum_lv_diff[:], op=ALU.subtract)
-        kl_sum = keep.tile([P, B_TILES], F32)
-        nc.vector.tensor_reduce(out=kl_sum[:], in_=kl_parts[:], axis=AXIS.X, op=ALU.add)
-        nc.vector.tensor_scalar(
-            out=kl_cols[:, 0:B_TILES], in0=kl_sum[:], scalar1=0.5, scalar2=-0.5 * Z, op0=ALU.mult, op1=ALU.add
-        )
         kl_bank = psum_t.tile([P, 4 * P], F32, tag="bank")
-        nc.tensor.transpose(out=kl_bank[:, 0:P], in_=kl_cols[:], identity=ident[:])
+        for j in range(KL_TERMS * Z_PARTS):
+            nc.tensor.matmul(
+                out=kl_bank[:, 0:P],
+                lhsT=kl_sums[:, j, :],
+                rhs=ident[:],
+                start=(j == 0),
+                stop=(j == KL_TERMS * Z_PARTS - 1),
+            )
         kl_rows = keep.tile([P, P], F32)
-        nc.vector.tensor_copy(out=kl_rows[:], in_=kl_bank[:, 0:P])
+        nc.scalar.activation(out=kl_rows[:], in_=kl_bank[:, 0:P], func=ACT.Copy, scale=0.5, bias=-0.5 * Z)
         nc.sync.dma_start(out=out_3.rearrange("(t p) -> t p", p=P), in_=kl_rows[0:B_TILES, :])

@@ -149,7 +149,7 @@ def tile_vrnncell_pa_kernel(
         def prepare_w1(c):
             banks = [transpose_pass(w1_words[c], g) for g in range(PASSES1)]
             grouped = [
-                group_rows_even_odd(nc.vector.tensor_copy if g == 0 else nc.scalar.copy, banks[g])
+                group_rows_even_odd(nc.vector.tensor_copy if g == PASSES1 - 1 else nc.scalar.copy, banks[g])
                 for g in range(PASSES1)
             ]
             for g in range(PASSES1):
@@ -209,15 +209,17 @@ def tile_vrnncell_pa_kernel(
         def kl_sum(term, part, t):
             return kl_sums[:, term * Z_PARTS + part, t : t + 1]
 
-        def prepare_w2(q):
+        def group_w2(q):
             banks = [transpose_pass(w2_words[q], g) for g in range(PASSES2)]
-            vector_helps = q < PREPARE_AHEAD
-            grouped = [
-                group_rows_in_order(nc.vector.tensor_copy if vector_helps and g == 0 else nc.scalar.copy, banks[g])
-                for g in range(PASSES2)
-            ]
+            return [group_rows_in_order(nc.scalar.copy, banks[g]) for g in range(PASSES2)]
+
+        def quantise_w2(q, g, grouped):
+            quantise(grouped[g], w2_codes[:, q, g, :], w2_scales[:, q, g, :])
+
+        def prepare_w2(q):
+            grouped = group_w2(q)
             for g in range(PASSES2):
-                quantise(grouped[g], w2_codes[:, q, g, :], w2_scales[:, q, g, :])
+                quantise_w2(q, g, grouped)
 
         def layer2(q):
             stats_acc = psum_acc.tile([P, B_TILES, PAIR], F32, tag="acc")
@@ -240,13 +242,6 @@ def tile_vrnncell_pa_kernel(
         def store(out, tile, cols):
             nc.sync.dma_start(out=out.rearrange("(t p) z -> p t z", p=P)[:, :, cols], in_=tile[:, :, cols])
 
-        def finish_mu(part, stats_acc):
-            cols = slice(part * PAIR, (part + 1) * PAIR)
-            nc.vector.tensor_tensor(out=mu_q[:, :, cols], in0=stats_acc[:], in1=bias2(part), op=ALU.add)
-            store(out_1, mu_q, cols)
-            nc.vector.tensor_tensor(out=dev[:, :, cols], in0=mu_q[:, :, cols], in1=mup_sb[:, :, cols], op=ALU.subtract)
-            nc.vector.tensor_tensor(out=dev[:, :, cols], in0=dev[:, :, cols], in1=inv_std_p[:, :, cols], op=ALU.mult)
-
         def sum_dev_squares(part):
             cols = slice(part * PAIR, (part + 1) * PAIR)
             for t in range(B_TILES):
@@ -257,67 +252,71 @@ def tile_vrnncell_pa_kernel(
                     accum_out=kl_sum(DEV_SQ, part, t),
                 )
 
-        def clip_logvar(part, stats_acc):
+        def finish_mu(part):
             cols = slice(part * PAIR, (part + 1) * PAIR)
-            nc.vector.tensor_tensor(
-                out=lv_q[:, :, cols], in0=stats_acc[:], in1=bias2(Z_PARTS + part), op=ALU.add
-            )
-            nc.vector.tensor_scalar(
-                out=lv_q[:, :, cols], in0=lv_q[:, :, cols], scalar1=CLAMP, scalar2=-CLAMP, op0=ALU.min, op1=ALU.max
-            )
-            store(out_2, lv_q, cols)
-            nc.scalar.activation(out=std_q[:, :, cols], in_=lv_q[:, :, cols], func=ACT.Exp, scale=0.5)
-
-        def sum_logvar_terms(part):
-            cols = slice(part * PAIR, (part + 1) * PAIR)
-            for t in range(B_TILES):
-                nc.vector.scalar_tensor_tensor(
-                    out=lv_diff[:, t, cols],
-                    in0=lv_q[:, t, cols],
-                    scalar=-1.0,
-                    in1=lvp_sb[:, t, cols],
-                    op0=ALU.mult,
-                    op1=ALU.add,
-                    accum_out=kl_sum(LV_DIFF, part, t),
-                )
-            for t in range(B_TILES):
-                nc.scalar.activation(
-                    out=var_ratio[:, t, cols],
-                    in_=lv_diff[:, t, cols],
-                    func=ACT.Exp,
-                    scale=-1.0,
-                    accum_out=kl_sum(VAR_RATIO, part, t),
-                )
-
-        def sample(part):
-            cols = slice(part * PAIR, (part + 1) * PAIR)
-            nc.vector.tensor_tensor(out=z_sb[:, :, cols], in0=std_q[:, :, cols], in1=eps_sb[:, :, cols], op=ALU.mult)
-            nc.vector.tensor_tensor(out=z_sb[:, :, cols], in0=z_sb[:, :, cols], in1=mu_q[:, :, cols], op=ALU.add)
-            store(out_0, z_sb, cols)
-
-        def finish(q):
-            stats_acc = layer2(q)
-            if 1 <= q <= Z_PARTS:
-                sum_dev_squares(q - 1)
-            if q > Z_PARTS:
-                sum_logvar_terms(q - Z_PARTS - 1)
-            if q < Z_PARTS:
-                finish_mu(q, stats_acc)
-            else:
-                clip_logvar(q - Z_PARTS, stats_acc)
-
-        for q in range(W2_PAIRS + PREPARE_AHEAD):
-            if q < W2_PAIRS:
-                prepare_w2(q)
-            if q == 0:
-                layer1_and_quantise(W1_PAIRS - 1)
-            if q == PREPARE_AHEAD:
+            q_ahead = part + PREPARE_AHEAD
+            grouped = group_w2(q_ahead)
+            if part == 0:
                 nc.scalar.activation(out=inv_std_p[:], in_=lvp_sb[:], func=ACT.Exp, scale=-0.5)
-            if q >= PREPARE_AHEAD:
-                finish(q - PREPARE_AHEAD)
-        sum_logvar_terms(Z_PARTS - 1)
+            stats_acc = layer2(part)
+            if part > 0:
+                sum_dev_squares(part - 1)
+            quantise_w2(q_ahead, 0, grouped)
+            nc.vector.tensor_tensor(out=mu_q[:, :, cols], in0=stats_acc[:], in1=bias2(part), op=ALU.add)
+            store(out_1, mu_q, cols)
+            quantise_w2(q_ahead, 1, grouped)
+            nc.vector.tensor_tensor(out=dev[:, :, cols], in0=mu_q[:, :, cols], in1=mup_sb[:, :, cols], op=ALU.subtract)
+            quantise_w2(q_ahead, 2, grouped)
+            nc.vector.tensor_tensor(out=dev[:, :, cols], in0=dev[:, :, cols], in1=inv_std_p[:, :, cols], op=ALU.mult)
+
+        def finish_logvar_and_sample():
+            parts = range(Z_PARTS)
+            col_ranges = [slice(part * PAIR, (part + 1) * PAIR) for part in parts]
+            stats_accs = [layer2(Z_PARTS + part) for part in parts]
+            sum_dev_squares(Z_PARTS - 1)
+            for part in parts:
+                nc.vector.tensor_tensor(
+                    out=lv_q[:, :, col_ranges[part]], in0=stats_accs[part][:], in1=bias2(Z_PARTS + part), op=ALU.add
+                )
+            for cols in col_ranges:
+                nc.vector.tensor_scalar(
+                    out=lv_q[:, :, cols], in0=lv_q[:, :, cols], scalar1=CLAMP, scalar2=-CLAMP, op0=ALU.min, op1=ALU.max
+                )
+                store(out_2, lv_q, cols)
+                nc.scalar.activation(out=std_q[:, :, cols], in_=lv_q[:, :, cols], func=ACT.Exp, scale=0.5)
+            for part in parts:
+                for t in range(B_TILES):
+                    nc.vector.scalar_tensor_tensor(
+                        out=lv_diff[:, t, col_ranges[part]],
+                        in0=lv_q[:, t, col_ranges[part]],
+                        scalar=-1.0,
+                        in1=lvp_sb[:, t, col_ranges[part]],
+                        op0=ALU.mult,
+                        op1=ALU.add,
+                        accum_out=kl_sum(LV_DIFF, part, t),
+                    )
+            for part in parts:
+                for t in range(B_TILES):
+                    nc.scalar.activation(
+                        out=var_ratio[:, t, col_ranges[part]],
+                        in_=lv_diff[:, t, col_ranges[part]],
+                        func=ACT.Exp,
+                        scale=-1.0,
+                        accum_out=kl_sum(VAR_RATIO, part, t),
+                    )
+            for cols in col_ranges:
+                nc.vector.tensor_tensor(out=z_sb[:, :, cols], in0=std_q[:, :, cols], in1=eps_sb[:, :, cols], op=ALU.mult)
+            for cols in col_ranges:
+                nc.vector.tensor_tensor(out=z_sb[:, :, cols], in0=z_sb[:, :, cols], in1=mu_q[:, :, cols], op=ALU.add)
+                store(out_0, z_sb, cols)
+
+        assert PREPARE_AHEAD == Z_PARTS
+        prepare_w2(0)
+        layer1_and_quantise(W1_PAIRS - 1)
+        prepare_w2(1)
         for part in range(Z_PARTS):
-            sample(part)
+            finish_mu(part)
+        finish_logvar_and_sample()
 
         kl_bank = psum_t.tile([P, 4 * P], F32, tag="bank")
         for j in range(KL_TERMS * Z_PARTS):

@@ -177,23 +177,26 @@ def tile_vrnncell_pa_kernel(
                 )
 
         def quantise_hid(g):
-            hid_grouped = stage.tile([P, 4 * B], BF16, align_bytes=64, tag="grouped")
-            nc.vector.tensor_copy(
-                out=hid_grouped[:].rearrange("p (b t) -> p b t", t=4),
-                in_=hid_rows[:, 4 * g : 4 * g + 4, :].rearrange("p t b -> p b t"),
-            )
-            quantise(hid_grouped, hid_codes[:, g, :], hid_scales[:, g, :])
+            hid_grouped = stage.tile([P, B_TILES, P, 4], BF16, align_bytes=64, tag="grouped")
+            for bt in range(B_TILES):
+                nc.vector.tensor_copy(
+                    out=hid_grouped[:, bt, :, :],
+                    in_=hid_rows[:, 4 * g : 4 * g + 4, bt * P : (bt + 1) * P].rearrange("p t b -> p b t"),
+                )
+            for bt in range(B_TILES):
+                nc.vector.quantize_mx(
+                    out=hid_codes[:, g, bt * P : (bt + 1) * P].bitcast(FP8X4),
+                    scales=hid_scales[:, g, bt * P : (bt + 1) * P],
+                    in_=hid_grouped[:, bt, :, :].rearrange("p b t -> p (b t)"),
+                )
 
-        def layer1_and_quantise(c):
-            layer1(c)
-            if c % 2 == 1:
-                quantise_hid(c // 2)
-
-        for c in range(W1_PAIRS + PREPARE_AHEAD - 1):
-            if c < W1_PAIRS:
-                prepare_w1(c)
-            if c >= PREPARE_AHEAD:
-                layer1_and_quantise(c - PREPARE_AHEAD)
+        for g in range(PASSES2):
+            prepare_w1(2 * g)
+            prepare_w1(2 * g + 1)
+            if g > 0:
+                layer1(2 * g - 1)
+                quantise_hid(g - 1)
+            layer1(2 * g)
 
         inv_std_p = keep.tile([P, B_TILES, Z], F32)
 
@@ -312,7 +315,8 @@ def tile_vrnncell_pa_kernel(
 
         assert PREPARE_AHEAD == Z_PARTS
         prepare_w2(0)
-        layer1_and_quantise(W1_PAIRS - 1)
+        layer1(W1_PAIRS - 1)
+        quantise_hid(PASSES2 - 1)
         prepare_w2(1)
         for part in range(Z_PARTS):
             finish_mu(part)

@@ -40,7 +40,6 @@ def tile_vrnncell_pa_kernel(
         stage = ctx.enter_context(tc.tile_pool(name="stage", bufs=6))
         psum_t = ctx.enter_context(tc.psum_pool(name="psum_t", bufs=6))
         psum_acc = ctx.enter_context(tc.psum_pool(name="psum_acc", bufs=2))
-        ctx.enter_context(tc.manual_schedule())
 
         def load_pair(rows, width, name):
             raw = keep.tile([P, 2 * width], BF16, name=name)

from contextlib import ExitStack

import concourse.mybir as mybir
from concourse.masks import make_identity

F32 = mybir.dt.float32
BF16 = mybir.dt.bfloat16
U32 = mybir.dt.uint32
U8 = mybir.dt.uint8
FP8X4 = mybir.dt.float8_e4m3fn_x4
ACT = mybir.ActivationFunctionType
ALU = mybir.AluOpType

P = 128
K_PASS = 4 * P
PAIR = 2 * P

B, O, H, Z = 256, 512, 1536, 512
K1 = O + H
PASSES1 = K1 // K_PASS
PASSES2 = H // K_PASS
W1_PAIRS = H // PAIR
W2_PAIRS = 2 * Z // PAIR
B_TILES = B // P
Z_PARTS = Z // PAIR
CLAMP = 10.0
PREPARE_AHEAD = 2
KL_TERMS = 3
DEV_SQ, LV_DIFF, VAR_RATIO = 0, 1, 2

FLOPS = 2 * B * K1 * H + 2 * B * H * 2 * Z


def tile_vrnncell_pa_kernel(
    tc, x_t, h_prev, eps, enc_w1, enc_b1, enc_w2, enc_b2, mu_p, logvar_p, out_0, out_1, out_2, out_3
):
    nc = tc.nc
    with ExitStack() as ctx:
        keep = ctx.enter_context(tc.tile_pool(name="keep", bufs=1))
        stage = ctx.enter_context(tc.tile_pool(name="stage", bufs=6))
        psum_t = ctx.enter_context(tc.psum_pool(name="psum_t", bufs=6))
        psum_acc = ctx.enter_context(tc.psum_pool(name="psum_acc", bufs=2))

        def load_pair(rows, width, name):
            raw = keep.tile([P, 2 * width], BF16, name=name)
            nc.sync.dma_start(out=raw[:], in_=rows.rearrange("(p a) k -> p (a k)", a=2))
            return raw[:].bitcast(F32).rearrange("p (a w) -> p a w", a=2)

        x_words = load_pair(x_t, O, "x_raw")
        h_words = load_pair(h_prev, H, "h_raw")
        w1_words = [
            load_pair(enc_w1[c * PAIR : (c + 1) * PAIR, :], K1, "w1_raw%d" % c) for c in range(W1_PAIRS)
        ]

        def load_prior(src, name):
            prior = keep.tile([P, B_TILES, Z], BF16, name=name)
            nc.sync.dma_start(out=prior[:], in_=src.rearrange("(t p) z -> p t z", p=P))
            return prior

        lvp_sb = load_prior(logvar_p, "lvp_sb")
        mup_sb = load_prior(mu_p, "mup_sb")
        eps_sb = load_prior(eps, "eps_sb")
        w2_words = [
            load_pair(enc_w2[q * PAIR : (q + 1) * PAIR, :], H, "w2_raw%d" % q) for q in range(W2_PAIRS)
        ]

        ident = keep.tile([P, P], F32)
        make_identity(nc, ident[:])
        ones = keep.tile([P, P], BF16)
        nc.gpsimd.memset(ones[:], 1.0)
        b1_rows = keep.tile([P, P], F32)
        nc.gpsimd.memset(b1_rows[:], 0.0)
        nc.scalar.dma_start(
            out=b1_rows[:].bitcast(BF16)[0:W1_PAIRS, :], in_=enc_b1.rearrange("(c w) -> c w", c=W1_PAIRS)
        )
        b2_row = keep.tile([P, 2 * Z], BF16)
        nc.gpsimd.memset(b2_row[:], 0.0)
        nc.scalar.dma_start(out=b2_row[0:1, :], in_=enc_b2.rearrange("(o n) -> o n", o=1))
        kl_sums = keep.tile([P, KL_TERMS * Z_PARTS, P], F32)
        nc.gpsimd.memset(kl_sums[:], 0.0)

        warm = keep.tile([P, 1], F32)
        nc.vector.memset(warm[:], 0.0)
        nc.scalar.activation(out=warm[:], in_=warm[:], func=ACT.Exp)

        x_codes = keep.tile([P, PASSES1, B], U32, align_bytes=64)
        x_scales = keep.tile([P, PASSES1, B], U8, align_bytes=64)
        w1_codes = keep.tile([P, W1_PAIRS, PASSES1, PAIR], U32, align_bytes=64)
        w1_scales = keep.tile([P, W1_PAIRS, PASSES1, PAIR], U8, align_bytes=64)
        hid_codes = keep.tile([P, PASSES2, B], U32, align_bytes=64)
        hid_scales = keep.tile([P, PASSES2, B], U8, align_bytes=64)
        w2_codes = keep.tile([P, W2_PAIRS, PASSES2, PAIR], U32, align_bytes=64)
        w2_scales = keep.tile([P, W2_PAIRS, PASSES2, PAIR], U8, align_bytes=64)

        def transpose_pass(words, g):
            bank = psum_t.tile([P, 4 * P], F32)
            for a in range(2):
                for u in range(2):
                    nc.tensor.transpose(
                        out=bank[:, (2 * a + u) * P : (2 * a + u + 1) * P],
                        in_=words[:, a, (2 * g + u) * P : (2 * g + u + 1) * P],
                        identity=ident[:],
                    )
            return bank

        def group_rows_in_order(copy, bank):
            grouped = stage.tile([P, 4 * PAIR], BF16, align_bytes=64)
            copy(
                out=grouped[:].bitcast(F32).rearrange("p (r a u) -> p r a u", a=2, u=2),
                in_=bank[:].rearrange("p (a u r) -> p r a u", a=2, u=2),
            )
            return grouped

        def group_rows_even_odd(copy, bank):
            grouped = stage.tile([P, 4 * PAIR], BF16, align_bytes=64)
            copy(
                out=grouped[:].bitcast(F32).rearrange("p (a r u) -> p a r u", a=2, u=2),
                in_=bank[:].rearrange("p (a u r) -> p a r u", a=2, u=2),
            )
            return grouped

        def quantise(grouped, codes, scales):
            nc.vector.quantize_mx(out=codes.bitcast(FP8X4), scales=scales, in_=grouped[:])

        x_banks = [transpose_pass(x_words, 0)] + [transpose_pass(h_words, g) for g in range(PASSES1 - 1)]
        x_grouped = [
            group_rows_in_order(nc.vector.tensor_copy if g % 2 == 0 else nc.scalar.copy, x_banks[g])
            for g in range(PASSES1)
        ]
        for g in range(PASSES1):
            quantise(x_grouped[g], x_codes[:, g, :], x_scales[:, g, :])

        b1_bank = psum_t.tile([P, 4 * P], F32, tag="bank")
        nc.tensor.transpose(out=b1_bank[:, 0:P], in_=b1_rows[:], identity=ident[:])
        b1_cols = keep.tile([P, 2 * W1_PAIRS], F32)
        nc.vector.tensor_copy(out=b1_cols[:], in_=b1_bank[:].bitcast(BF16)[:, 0 : 2 * W1_PAIRS])

        b2_all = keep.tile([P, 2 * Z], F32)
        for half in range(2):
            b2_bank = psum_acc.tile([P, Z], F32, tag="acc")
            nc.tensor.matmul(
                out=b2_bank[:], lhsT=ones[:], rhs=b2_row[:, half * Z : (half + 1) * Z], start=True, stop=True
            )
            nc.vector.tensor_copy(out=b2_all[:, half * Z : (half + 1) * Z], in_=b2_bank[:])

        hid_rows = keep.tile([P, 2 * W1_PAIRS, B], BF16)

        def prepare_w1(c):
            banks = [transpose_pass(w1_words[c], g) for g in range(PASSES1)]
            grouped = [
                group_rows_even_odd(nc.vector.tensor_copy if g == PASSES1 - 1 else nc.scalar.copy, banks[g])
                for g in range(PASSES1)
            ]
            for g in range(PASSES1):
                quantise(grouped[g], w1_codes[:, c, g, :], w1_scales[:, c, g, :])

        def layer1(c):
            hid_acc = psum_acc.tile([P, 2, B], F32, tag="acc")
            for e in range(2):
                for g in range(PASSES1):
                    nc.tensor.matmul_mx(
                        out=hid_acc[:, e, :],
                        lhsT=w1_codes[:, c, g, e * P : (e + 1) * P].bitcast(FP8X4),
                        lhsT_scale=w1_scales[:, c, g, e * P : (e + 1) * P],
                        rhs=x_codes[:, g, :].bitcast(FP8X4),
                        rhs_scale=x_scales[:, g, :],
                        start=(g == 0),
                        stop=(g == PASSES1 - 1),
                    )
            for e in range(2):
                nc.scalar.activation(
                    out=hid_rows[:, 2 * c + e, :],
                    in_=hid_acc[:, e, :],
                    func=ACT.Relu,
                    bias=b1_cols[:, 2 * c + e : 2 * c + e + 1],
                )

        def quantise_hid(g):
            hid_grouped = stage.tile([P, B_TILES, P, 4], BF16, align_bytes=64, tag="grouped")
            for bt in range(B_TILES):
                nc.vector.tensor_copy(
                    out=hid_grouped[:, bt, :, :],
                    in_=hid_rows[:, 4 * g : 4 * g + 4, bt * P : (bt + 1) * P].rearrange("p t b -> p b t"),
                )
            for bt in range(B_TILES):
                nc.vector.quantize_mx(
                    out=hid_codes[:, g, bt * P : (bt + 1) * P].bitcast(FP8X4),
                    scales=hid_scales[:, g, bt * P : (bt + 1) * P],
                    in_=hid_grouped[:, bt, :, :].rearrange("p b t -> p (b t)"),
                )

        for g in range(PASSES2):
            prepare_w1(2 * g)
            prepare_w1(2 * g + 1)
            if g > 0:
                layer1(2 * g - 1)
                quantise_hid(g - 1)
            layer1(2 * g)

        inv_std_p = keep.tile([P, B_TILES, Z], F32)

        mu_q = keep.tile([P, B_TILES, Z], F32)
        lv_q = keep.tile([P, B_TILES, Z], F32)
        std_q = keep.tile([P, B_TILES, Z], F32)
        z_sb = keep.tile([P, B_TILES, Z], F32)
        dev = keep.tile([P, B_TILES, Z], F32)
        lv_diff = keep.tile([P, B_TILES, Z], F32)
        dev_sq = keep.tile([P, B_TILES, Z], BF16)
        var_ratio = keep.tile([P, B_TILES, Z], BF16)

        def kl_sum(term, part, t):
            return kl_sums[:, term * Z_PARTS + part, t : t + 1]

        def group_w2(q):
            banks = [transpose_pass(w2_words[q], g) for g in range(PASSES2)]
            return [group_rows_in_order(nc.scalar.copy, banks[g]) for g in range(PASSES2)]

        def quantise_w2(q, g, grouped):
            quantise(grouped[g], w2_codes[:, q, g, :], w2_scales[:, q, g, :])

        def prepare_w2(q):
            grouped = group_w2(q)
            for g in range(PASSES2):
                quantise_w2(q, g, grouped)

        def layer2(q):
            stats_acc = psum_acc.tile([P, B_TILES, PAIR], F32, tag="acc")
            for t in range(B_TILES):
                for g in range(PASSES2):
                    nc.tensor.matmul_mx(
                        out=stats_acc[:, t, :],
                        lhsT=hid_codes[:, g, t * P : (t + 1) * P].bitcast(FP8X4),
                        lhsT_scale=hid_scales[:, g, t * P : (t + 1) * P],
                        rhs=w2_codes[:, q, g, :].bitcast(FP8X4),
                        rhs_scale=w2_scales[:, q, g, :],
                        start=(g == 0),
                        stop=(g == PASSES2 - 1),
                    )
            return stats_acc

        def bias2(q):
            return b2_all[:, q * PAIR : (q + 1) * PAIR].unsqueeze(1).to_broadcast([P, B_TILES, PAIR])

        def store(out, tile, cols):
            nc.sync.dma_start(out=out.rearrange("(t p) z -> p t z", p=P)[:, :, cols], in_=tile[:, :, cols])

        def sum_dev_squares(part):
            cols = slice(part * PAIR, (part + 1) * PAIR)
            for t in range(B_TILES):
                nc.scalar.activation(
                    out=dev_sq[:, t, cols],
                    in_=dev[:, t, cols],
                    func=ACT.Square,
                    accum_out=kl_sum(DEV_SQ, part, t),
                )

        def finish_mu(part):
            cols = slice(part * PAIR, (part + 1) * PAIR)
            q_ahead = part + PREPARE_AHEAD
            grouped = group_w2(q_ahead)
            if part == 0:
                nc.scalar.activation(out=inv_std_p[:], in_=lvp_sb[:], func=ACT.Exp, scale=-0.5)
            stats_acc = layer2(part)
            if part > 0:
                sum_dev_squares(part - 1)
            quantise_w2(q_ahead, 0, grouped)
            nc.vector.tensor_tensor(out=mu_q[:, :, cols], in0=stats_acc[:], in1=bias2(part), op=ALU.add)
            store(out_1, mu_q, cols)
            quantise_w2(q_ahead, 1, grouped)
            nc.vector.tensor_tensor(out=dev[:, :, cols], in0=mu_q[:, :, cols], in1=mup_sb[:, :, cols], op=ALU.subtract)
            quantise_w2(q_ahead, 2, grouped)
            nc.vector.tensor_tensor(out=dev[:, :, cols], in0=dev[:, :, cols], in1=inv_std_p[:, :, cols], op=ALU.mult)

        def finish_logvar_and_sample():
            parts = range(Z_PARTS)
            col_ranges = [slice(part * PAIR, (part + 1) * PAIR) for part in parts]
            stats_accs = [layer2(Z_PARTS + part) for part in parts]
            sum_dev_squares(Z_PARTS - 1)
            for part in parts:
                nc.vector.tensor_tensor(
                    out=lv_q[:, :, col_ranges[part]], in0=stats_accs[part][:], in1=bias2(Z_PARTS + part), op=ALU.add
                )
            for cols in col_ranges:
                nc.vector.tensor_scalar(
                    out=lv_q[:, :, cols], in0=lv_q[:, :, cols], scalar1=CLAMP, scalar2=-CLAMP, op0=ALU.min, op1=ALU.max
                )
                store(out_2, lv_q, cols)
                nc.scalar.activation(out=std_q[:, :, cols], in_=lv_q[:, :, cols], func=ACT.Exp, scale=0.5)
            for part in parts:
                for t in range(B_TILES):
                    nc.vector.scalar_tensor_tensor(
                        out=lv_diff[:, t, col_ranges[part]],
                        in0=lv_q[:, t, col_ranges[part]],
                        scalar=-1.0,
                        in1=lvp_sb[:, t, col_ranges[part]],
                        op0=ALU.mult,
                        op1=ALU.add,
                        accum_out=kl_sum(LV_DIFF, part, t),
                    )
            for part in parts:
                for t in range(B_TILES):
                    nc.scalar.activation(
                        out=var_ratio[:, t, col_ranges[part]],
                        in_=lv_diff[:, t, col_ranges[part]],
                        func=ACT.Exp,
                        scale=-1.0,
                        accum_out=kl_sum(VAR_RATIO, part, t),
                    )
            for cols in col_ranges:
                nc.vector.tensor_tensor(out=z_sb[:, :, cols], in0=std_q[:, :, cols], in1=eps_sb[:, :, cols], op=ALU.mult)
            for cols in col_ranges:
                nc.vector.tensor_tensor(out=z_sb[:, :, cols], in0=z_sb[:, :, cols], in1=mu_q[:, :, cols], op=ALU.add)
                store(out_0, z_sb, cols)

        assert PREPARE_AHEAD == Z_PARTS
        prepare_w2(0)
        layer1(W1_PAIRS - 1)
        quantise_hid(PASSES2 - 1)
        prepare_w2(1)
        for part in range(Z_PARTS):
            finish_mu(part)
        finish_logvar_and_sample()

        kl_bank = psum_t.tile([P, 4 * P], F32, tag="bank")
        for j in range(KL_TERMS * Z_PARTS):
            nc.tensor.matmul(
                out=kl_bank[:, 0:P],
                lhsT=kl_sums[:, j, :],
                rhs=ident[:],
                start=(j == 0),
                stop=(j == KL_TERMS * Z_PARTS - 1),
            )
        kl_rows = keep.tile([P, P], F32)
        nc.scalar.activation(out=kl_rows[:], in_=kl_bank[:, 0:P], func=ACT.Copy, scale=0.5, bias=-0.5 * Z)
        nc.sync.dma_start(out=out_3.rearrange("(t p) -> t p", p=P), in_=kl_rows[0:B_TILES, :])
